import numpy as np
import ml_dtypes

BF16 = ml_dtypes.bfloat16


def bf(x):
    return np.asarray(x, np.float32).astype(BF16)


def f32(x):
    return np.asarray(x, np.float32)


def f64(x):
    return np.asarray(x).astype(np.float64)


def striped(idx):
    return np.tile(idx.reshape(-1, 16).T, (8, 1))


D, S, M, N, R = 128, 256, 256, 384, 16
SCALE = 0.25


def setup_inputs():
    mix = np.random.standard_normal((D, R)) * (SCALE / np.sqrt(R))
    return {"table": bf(mix @ np.random.standard_normal((R, S))), "w": bf(mix @ np.random.standard_normal((R, M))), "offs": striped(np.random.permutation(np.tile(np.arange(S), 2))[:N])}


def reference(table, w, offs):
    idx = offs[:16].T.reshape(-1)
    t = f64(table)[:, idx]
    q = f64(w)
    dot = q.T @ t
    qn = np.sqrt(np.sum(q * q, axis=0))[:, None]
    tn = np.sqrt(np.sum(t * t, axis=0))[None, :]
    return dot / (qn * tn)

@@ -1,0 +1,86 @@
+import concourse.mybir as mybir
+from concourse.masks import make_identity
+
+P = 128
+S = 256
+M = 256
+N = 384
+BLOCKS = M // P
+PIECE = 192
+PIECES = N // PIECE
+PIECE_COLS = PIECE // 16
+WARM_MATMULS = 24
+WARM_COLS = 64
+FLOPS = 2 * P * M * N
+
+BF16, F32, U16 = mybir.dt.bfloat16, mybir.dt.float32, mybir.dt.uint16
+FUNC = mybir.ActivationFunctionType
+MULT = mybir.AluOpType.mult
+
+
+def tile_model_kernel(tc, table, w, offs, out):
+    nc = tc.nc
+    with (
+        tc.tile_pool(name="held", bufs=1) as held,
+        tc.psum_pool(name="psum", bufs=1) as psum,
+    ):
+        w_sb = held.tile([P, M], BF16, name="w_sb")
+        nc.sync.dma_start(w_sb[:], w)
+        offsets = held.tile([P, N // 16], U16, name="offsets")
+        nc.sync.dma_start(offsets[:], offs)
+        table_sb = held.tile([P, S], BF16, name="table_sb")
+        nc.scalar.dma_start(table_sb[:], table)
+
+        ones = held.tile([P, P], BF16, name="ones")
+        nc.vector.memset(ones[:], 1.0)
+        identity = held.tile([P, P], BF16, name="identity")
+        make_identity(nc, identity[:])
+
+        unused_sb = held.tile([P, 1], F32, name="unused_sb")
+        nc.scalar.activation(unused_sb[:], ones[:, 0:1], FUNC.Abs_reciprocal_sqrt)
+        unused_ps = psum.tile([P, WARM_COLS], F32, name="unused_ps")
+        for i in range(WARM_MATMULS):
+            nc.tensor.matmul(unused_ps[:], ones[:], ones[:, :WARM_COLS], start=True, stop=True)
+
+        gram_ps = psum.tile([P, BLOCKS, P], F32, name="gram_ps")
+        for b in range(BLOCKS):
+            w_block = w_sb[:, b * P : (b + 1) * P]
+            nc.tensor.matmul(gram_ps[:, b, :], w_block, w_block, start=True, stop=True)
+
+        pieces = [offsets[:, p * PIECE_COLS : (p + 1) * PIECE_COLS] for p in range(PIECES)]
+        tail_ps = [psum.tile([P, 2, PIECE], F32, name=f"tail_ps{p}") for p in range(PIECES)]
+        dot = [[psum.tile([P, PIECE], F32, name=f"dot{p}_{b}") for b in range(BLOCKS)] for p in range(PIECES)]
+        for p in range(PIECES):
+            nc.tensor.matmul(
+                tail_ps[p][:, 0, :], identity[:], table_sb[:].indirect(pieces[p]), start=True, stop=True
+            )
+        for p in range(PIECES):
+            for b in range(BLOCKS):
+                nc.tensor.matmul(
+                    dot[p][b][:], w_sb[:, b * P : (b + 1) * P], table_sb[:].indirect(pieces[p]), start=True, stop=True
+                )
+
+        diagonal = held.tile([P, BLOCKS, P], F32, name="diagonal")
+        nc.vector.tensor_tensor(
+            diagonal[:], gram_ps[:], identity[:].unsqueeze(1).to_broadcast([P, BLOCKS, P]), MULT
+        )
+        head_sq = held.tile([P, BLOCKS], F32, name="head_sq")
+        nc.vector.reduce_sum(head_sq[:], diagonal[:], axis=mybir.AxisListType.X)
+        head_inv = held.tile([P, BLOCKS], F32, name="head_inv")
+
+        tail_sq = [held.tile([P, PIECE], BF16, name=f"tail_sq{p}") for p in range(PIECES)]
+        tail_inv = [held.tile([P, PIECE], F32, name=f"tail_inv{p}") for p in range(PIECES)]
+        for p in range(PIECES):
+            nc.scalar.activation(tail_sq[p][:], tail_ps[p][:, 0, :], FUNC.Square)
+        nc.scalar.activation(head_inv[:], head_sq[:], FUNC.Abs_reciprocal_sqrt)
+        for p in range(PIECES):
+            nc.tensor.matmul(tail_ps[p][:, 1, :], ones[:], tail_sq[p][:], start=True, stop=True)
+            nc.scalar.activation(tail_inv[p][:], tail_ps[p][:, 1, :], FUNC.Abs_reciprocal_sqrt)
+
+        for p in range(PIECES):
+            for b in range(BLOCKS):
+                cos = held.tile([P, PIECE], F32, name=f"cos{p}_{b}")
+                nc.vector.scalar_tensor_tensor(
+                    cos[:], dot[p][b][:], head_inv[:, b : b + 1], tail_inv[p][:], MULT, MULT
+                )
+                nc.sync.dma_start(out[b * P : (b + 1) * P, p * PIECE : (p + 1) * PIECE], cos[:])

@@ -9,6 +9,7 @@ BLOCKS = M // P
 PIECE = 192
 PIECES = N // PIECE
 PIECE_COLS = PIECE // 16
+BANK = 512
 WARM_MATMULS = 24
 WARM_COLS = 64
 FLOPS = 2 * P * M * N
@@ -16,6 +17,8 @@ FLOPS = 2 * P * M * N
 BF16, F32, U16 = mybir.dt.bfloat16, mybir.dt.float32, mybir.dt.uint16
 FUNC = mybir.ActivationFunctionType
 MULT = mybir.AluOpType.mult
+
+assert BLOCKS == PIECES and BLOCKS * PIECE + P == BANK
 
 
 def tile_model_kernel(tc, table, w, offs, out):
@@ -42,14 +45,19 @@ def tile_model_kernel(tc, table, w, offs, out):
         for i in range(WARM_MATMULS):
             nc.tensor.matmul(unused_ps[:], ones[:], ones[:, :WARM_COLS], start=True, stop=True)
 
-        gram_ps = psum.tile([P, BLOCKS, P], F32, name="gram_ps")
+        bank = [psum.tile([P, BANK], F32, name=f"bank{i}") for i in range(PIECES)]
+
+        diagonal = held.tile([P, BLOCKS, P], F32, name="diagonal")
         for b in range(BLOCKS):
             w_block = w_sb[:, b * P : (b + 1) * P]
-            nc.tensor.matmul(gram_ps[:, b, :], w_block, w_block, start=True, stop=True)
+            nc.tensor.matmul(bank[b][:, BANK - P :], w_block, w_block, start=True, stop=True)
+        for b in range(BLOCKS):
+            nc.vector.tensor_tensor(diagonal[:, b, :], bank[b][:, BANK - P :], identity[:], MULT)
+        head_sq = held.tile([P, BLOCKS], F32, name="head_sq")
+        nc.vector.reduce_sum(head_sq[:], diagonal[:], axis=mybir.AxisListType.X)
 
         pieces = [offsets[:, p * PIECE_COLS : (p + 1) * PIECE_COLS] for p in range(PIECES)]
         tail_ps = [psum.tile([P, 2, PIECE], F32, name=f"tail_ps{p}") for p in range(PIECES)]
-        dot = [[psum.tile([P, PIECE], F32, name=f"dot{p}_{b}") for b in range(BLOCKS)] for p in range(PIECES)]
         for p in range(PIECES):
             nc.tensor.matmul(
                 tail_ps[p][:, 0, :], identity[:], table_sb[:].indirect(pieces[p]), start=True, stop=True
@@ -57,19 +65,16 @@ def tile_model_kernel(tc, table, w, offs, out):
         for p in range(PIECES):
             for b in range(BLOCKS):
                 nc.tensor.matmul(
-                    dot[p][b][:], w_sb[:, b * P : (b + 1) * P], table_sb[:].indirect(pieces[p]), start=True, stop=True
+                    bank[p][:, b * PIECE : (b + 1) * PIECE],
+                    w_sb[:, b * P : (b + 1) * P],
+                    table_sb[:].indirect(pieces[p]),
+                    start=True,
+                    stop=True,
                 )
-
-        diagonal = held.tile([P, BLOCKS, P], F32, name="diagonal")
-        nc.vector.tensor_tensor(
-            diagonal[:], gram_ps[:], identity[:].unsqueeze(1).to_broadcast([P, BLOCKS, P]), MULT
-        )
-        head_sq = held.tile([P, BLOCKS], F32, name="head_sq")
-        nc.vector.reduce_sum(head_sq[:], diagonal[:], axis=mybir.AxisListType.X)
-        head_inv = held.tile([P, BLOCKS], F32, name="head_inv")
 
         tail_sq = [held.tile([P, PIECE], BF16, name=f"tail_sq{p}") for p in range(PIECES)]
         tail_inv = [held.tile([P, PIECE], F32, name=f"tail_inv{p}") for p in range(PIECES)]
+        head_inv = held.tile([P, BLOCKS], F32, name="head_inv")
         for p in range(PIECES):
             nc.scalar.activation(tail_sq[p][:], tail_ps[p][:, 0, :], FUNC.Square)
         nc.scalar.activation(head_inv[:], head_sq[:], FUNC.Abs_reciprocal_sqrt)
@@ -81,6 +86,6 @@ def tile_model_kernel(tc, table, w, offs, out):
             for b in range(BLOCKS):
                 cos = held.tile([P, PIECE], F32, name=f"cos{p}_{b}")
                 nc.vector.scalar_tensor_tensor(
-                    cos[:], dot[p][b][:], head_inv[:, b : b + 1], tail_inv[p][:], MULT, MULT
+                    cos[:], bank[p][:, b * PIECE : (b + 1) * PIECE], head_inv[:, b : b + 1], tail_inv[p][:], MULT, MULT
                 )
                 nc.sync.dma_start(out[b * P : (b + 1) * P, p * PIECE : (p + 1) * PIECE], cos[:])

@@ -88,4 +88,5 @@ def tile_model_kernel(tc, table, w, offs, out):
                 nc.vector.scalar_tensor_tensor(
                     cos[:], bank[p][:, b * PIECE : (b + 1) * PIECE], head_inv[:, b : b + 1], tail_inv[p][:], MULT, MULT
                 )
-                nc.sync.dma_start(out[b * P : (b + 1) * P, p * PIECE : (p + 1) * PIECE], cos[:])
+                queue = nc.sync if b == 0 else nc.scalar
+                queue.dma_start(out[b * P : (b + 1) * P, p * PIECE : (p + 1) * PIECE], cos[:])

@@ -11,7 +11,7 @@ PIECES = N // PIECE
 PIECE_COLS = PIECE // 16
 BANK = 512
 WARM_MATMULS = 24
-WARM_COLS = 64
+WARM_COLS = 32
 FLOPS = 2 * P * M * N
 
 BF16, F32, U16 = mybir.dt.bfloat16, mybir.dt.float32, mybir.dt.uint16
@@ -88,5 +88,4 @@ def tile_model_kernel(tc, table, w, offs, out):
                 nc.vector.scalar_tensor_tensor(
                     cos[:], bank[p][:, b * PIECE : (b + 1) * PIECE], head_inv[:, b : b + 1], tail_inv[p][:], MULT, MULT
                 )
-                queue = nc.sync if b == 0 else nc.scalar
-                queue.dma_start(out[b * P : (b + 1) * P, p * PIECE : (p + 1) * PIECE], cos[:])
+                nc.sync.dma_start(out[b * P : (b + 1) * P, p * PIECE : (p + 1) * PIECE], cos[:])

@@ -10,8 +10,6 @@ PIECE = 192
 PIECES = N // PIECE
 PIECE_COLS = PIECE // 16
 BANK = 512
-WARM_MATMULS = 24
-WARM_COLS = 32
 FLOPS = 2 * P * M * N
 
 BF16, F32, U16 = mybir.dt.bfloat16, mybir.dt.float32, mybir.dt.uint16
@@ -41,9 +39,6 @@ def tile_model_kernel(tc, table, w, offs, out):
 
         unused_sb = held.tile([P, 1], F32, name="unused_sb")
         nc.scalar.activation(unused_sb[:], ones[:, 0:1], FUNC.Abs_reciprocal_sqrt)
-        unused_ps = psum.tile([P, WARM_COLS], F32, name="unused_ps")
-        for i in range(WARM_MATMULS):
-            nc.tensor.matmul(unused_ps[:], ones[:], ones[:, :WARM_COLS], start=True, stop=True)
 
         bank = [psum.tile([P, BANK], F32, name=f"bank{i}") for i in range(PIECES)]
 

@@ -26,7 +26,8 @@ def tile_model_kernel(tc, table, w, offs, out):
         tc.psum_pool(name="psum", bufs=1) as psum,
     ):
         w_sb = held.tile([P, M], BF16, name="w_sb")
-        nc.sync.dma_start(w_sb[:], w)
+        nc.sync.dma_start(w_sb[:, :P], w[:, :P])
+        nc.scalar.dma_start(w_sb[:, P:], w[:, P:])
         offsets = held.tile([P, N // 16], U16, name="offsets")
         nc.sync.dma_start(offsets[:], offs)
         table_sb = held.tile([P, S], BF16, name="table_sb")

@@ -10,13 +10,15 @@ PIECE = 192
 PIECES = N // PIECE
 PIECE_COLS = PIECE // 16
 BANK = 512
+PART = 128
+PARTS = N // PART
 FLOPS = 2 * P * M * N
 
 BF16, F32, U16 = mybir.dt.bfloat16, mybir.dt.float32, mybir.dt.uint16
 FUNC = mybir.ActivationFunctionType
 MULT = mybir.AluOpType.mult
 
-assert BLOCKS == PIECES and BLOCKS * PIECE + P == BANK
+assert N + P == BANK
 
 
 def tile_model_kernel(tc, table, w, offs, out):
@@ -41,7 +43,7 @@ def tile_model_kernel(tc, table, w, offs, out):
         unused_sb = held.tile([P, 1], F32, name="unused_sb")
         nc.scalar.activation(unused_sb[:], ones[:, 0:1], FUNC.Abs_reciprocal_sqrt)
 
-        bank = [psum.tile([P, BANK], F32, name=f"bank{i}") for i in range(PIECES)]
+        bank = [psum.tile([P, BANK], F32, name=f"bank{b}") for b in range(BLOCKS)]
 
         diagonal = held.tile([P, BLOCKS, P], F32, name="diagonal")
         for b in range(BLOCKS):
@@ -53,35 +55,36 @@ def tile_model_kernel(tc, table, w, offs, out):
         nc.vector.reduce_sum(head_sq[:], diagonal[:], axis=mybir.AxisListType.X)
 
         pieces = [offsets[:, p * PIECE_COLS : (p + 1) * PIECE_COLS] for p in range(PIECES)]
-        tail_ps = [psum.tile([P, 2, PIECE], F32, name=f"tail_ps{p}") for p in range(PIECES)]
+        picked = [psum.tile([P, PIECE], F32, name=f"picked{p}") for p in range(PIECES)]
         for p in range(PIECES):
-            nc.tensor.matmul(
-                tail_ps[p][:, 0, :], identity[:], table_sb[:].indirect(pieces[p]), start=True, stop=True
-            )
+            nc.tensor.matmul(picked[p][:], identity[:], table_sb[:].indirect(pieces[p]), start=True, stop=True)
         for p in range(PIECES):
             for b in range(BLOCKS):
                 nc.tensor.matmul(
-                    bank[p][:, b * PIECE : (b + 1) * PIECE],
+                    bank[b][:, p * PIECE : (p + 1) * PIECE],
                     w_sb[:, b * P : (b + 1) * P],
                     table_sb[:].indirect(pieces[p]),
                     start=True,
                     stop=True,
                 )
 
-        tail_sq = [held.tile([P, PIECE], BF16, name=f"tail_sq{p}") for p in range(PIECES)]
-        tail_inv = [held.tile([P, PIECE], F32, name=f"tail_inv{p}") for p in range(PIECES)]
+        tail_sq = held.tile([P, N], BF16, name="tail_sq")
+        for p in range(PIECES):
+            nc.scalar.activation(tail_sq[:, p * PIECE : (p + 1) * PIECE], picked[p][:], FUNC.Square)
         head_inv = held.tile([P, BLOCKS], F32, name="head_inv")
-        for p in range(PIECES):
-            nc.scalar.activation(tail_sq[p][:], tail_ps[p][:, 0, :], FUNC.Square)
         nc.scalar.activation(head_inv[:], head_sq[:], FUNC.Abs_reciprocal_sqrt)
-        for p in range(PIECES):
-            nc.tensor.matmul(tail_ps[p][:, 1, :], ones[:], tail_sq[p][:], start=True, stop=True)
-            nc.scalar.activation(tail_inv[p][:], tail_ps[p][:, 1, :], FUNC.Abs_reciprocal_sqrt)
 
-        for p in range(PIECES):
+        tail_inv = [held.tile([P, PART], F32, name=f"tail_inv{q}") for q in range(PARTS)]
+        for q in range(PARTS):
+            part = slice(q * PART, (q + 1) * PART)
+            sums = psum.tile([P, PART], F32, name=f"sums{q}")
+            nc.tensor.matmul(sums[:], ones[:], tail_sq[:, part], start=True, stop=True)
+            nc.scalar.activation(tail_inv[q][:], sums[:], FUNC.Abs_reciprocal_sqrt)
+        for q in range(PARTS):
+            part = slice(q * PART, (q + 1) * PART)
             for b in range(BLOCKS):
-                cos = held.tile([P, PIECE], F32, name=f"cos{p}_{b}")
+                cos = held.tile([P, PART], F32, name=f"cos{q}_{b}")
                 nc.vector.scalar_tensor_tensor(
-                    cos[:], bank[p][:, b * PIECE : (b + 1) * PIECE], head_inv[:, b : b + 1], tail_inv[p][:], MULT, MULT
+                    cos[:], bank[b][:, part], head_inv[:, b : b + 1], tail_inv[q][:], MULT, MULT
                 )
-                nc.sync.dma_start(out[b * P : (b + 1) * P, p * PIECE : (p + 1) * PIECE], cos[:])
+                nc.sync.dma_start(out[b * P : (b + 1) * P, part], cos[:])

@@ -10,8 +10,8 @@ PIECE = 192
 PIECES = N // PIECE
 PIECE_COLS = PIECE // 16
 BANK = 512
-PART = 128
-PARTS = N // PART
+FIRST = N // 3
+PARTS = [slice(0, FIRST), slice(FIRST, N)]
 FLOPS = 2 * P * M * N
 
 BF16, F32, U16 = mybir.dt.bfloat16, mybir.dt.float32, mybir.dt.uint16
@@ -74,16 +74,14 @@ def tile_model_kernel(tc, table, w, offs, out):
         head_inv = held.tile([P, BLOCKS], F32, name="head_inv")
         nc.scalar.activation(head_inv[:], head_sq[:], FUNC.Abs_reciprocal_sqrt)
 
-        tail_inv = [held.tile([P, PART], F32, name=f"tail_inv{q}") for q in range(PARTS)]
-        for q in range(PARTS):
-            part = slice(q * PART, (q + 1) * PART)
-            sums = psum.tile([P, PART], F32, name=f"sums{q}")
+        tail_inv = [held.tile([P, part.stop - part.start], F32, name=f"tail_inv{q}") for q, part in enumerate(PARTS)]
+        for q, part in enumerate(PARTS):
+            sums = psum.tile([P, part.stop - part.start], F32, name=f"sums{q}")
             nc.tensor.matmul(sums[:], ones[:], tail_sq[:, part], start=True, stop=True)
             nc.scalar.activation(tail_inv[q][:], sums[:], FUNC.Abs_reciprocal_sqrt)
-        for q in range(PARTS):
-            part = slice(q * PART, (q + 1) * PART)
+        for q, part in enumerate(PARTS):
             for b in range(BLOCKS):
-                cos = held.tile([P, PART], F32, name=f"cos{q}_{b}")
+                cos = held.tile([P, part.stop - part.start], F32, name=f"cos{q}_{b}")
                 nc.vector.scalar_tensor_tensor(
                     cos[:], bank[b][:, part], head_inv[:, b : b + 1], tail_inv[q][:], MULT, MULT
                 )

@@ -9,6 +9,7 @@ BLOCKS = M // P
 PIECE = 192
 PIECES = N // PIECE
 PIECE_COLS = PIECE // 16
+HALF = P // 2
 BANK = 512
 FIRST = N // 3
 PARTS = [slice(0, FIRST), slice(FIRST, N)]
@@ -18,7 +19,7 @@ BF16, F32, U16 = mybir.dt.bfloat16, mybir.dt.float32, mybir.dt.uint16
 FUNC = mybir.ActivationFunctionType
 MULT = mybir.AluOpType.mult
 
-assert N + P == BANK
+assert N + HALF < BANK
 
 
 def tile_model_kernel(tc, table, w, offs, out):
@@ -27,13 +28,13 @@ def tile_model_kernel(tc, table, w, offs, out):
         tc.tile_pool(name="held", bufs=1) as held,
         tc.psum_pool(name="psum", bufs=1) as psum,
     ):
-        w_sb = held.tile([P, M], BF16, name="w_sb")
-        nc.sync.dma_start(w_sb[:, :P], w[:, :P])
-        nc.scalar.dma_start(w_sb[:, P:], w[:, P:])
-        offsets = held.tile([P, N // 16], U16, name="offsets")
-        nc.sync.dma_start(offsets[:], offs)
+        w_sb = [held.tile([P, P], BF16, name=f"w_sb{b}") for b in range(BLOCKS)]
+        nc.sync.dma_start(w_sb[0][:], w[:, :P])
         table_sb = held.tile([P, S], BF16, name="table_sb")
         nc.scalar.dma_start(table_sb[:], table)
+        offsets = held.tile([P, N // 16], U16, name="offsets")
+        nc.sync.dma_start(offsets[:], offs)
+        nc.scalar.dma_start(w_sb[1][:], w[:, P:])
 
         ones = held.tile([P, P], BF16, name="ones")
         nc.vector.memset(ones[:], 1.0)
@@ -45,24 +46,27 @@ def tile_model_kernel(tc, table, w, offs, out):
 
         bank = [psum.tile([P, BANK], F32, name=f"bank{b}") for b in range(BLOCKS)]
 
-        diagonal = held.tile([P, BLOCKS, P], F32, name="diagonal")
+        diagonal = held.tile([P, P], F32, name="diagonal")
         for b in range(BLOCKS):
-            w_block = w_sb[:, b * P : (b + 1) * P]
-            nc.tensor.matmul(bank[b][:, BANK - P :], w_block, w_block, start=True, stop=True)
+            half = slice(b * HALF, (b + 1) * HALF)
+            nc.tensor.matmul(bank[b][:, N : N + HALF], w_sb[0][:], w_sb[0][:, half], start=True, stop=True)
         for b in range(BLOCKS):
-            nc.vector.tensor_tensor(diagonal[:, b, :], bank[b][:, BANK - P :], identity[:], MULT)
-        head_sq = held.tile([P, BLOCKS], F32, name="head_sq")
+            half = slice(b * HALF, (b + 1) * HALF)
+            nc.vector.tensor_tensor(diagonal[:, half], bank[b][:, N : N + HALF], identity[:, half], MULT)
+        head_sq = held.tile([P, 1], F32, name="head_sq")
         nc.vector.reduce_sum(head_sq[:], diagonal[:], axis=mybir.AxisListType.X)
+        w_sq = held.tile([P, P], BF16, name="w_sq")
+        nc.gpsimd.tensor_tensor(w_sq[:], w_sb[1][:], w_sb[1][:], MULT)
 
         pieces = [offsets[:, p * PIECE_COLS : (p + 1) * PIECE_COLS] for p in range(PIECES)]
         picked = [psum.tile([P, PIECE], F32, name=f"picked{p}") for p in range(PIECES)]
         for p in range(PIECES):
             nc.tensor.matmul(picked[p][:], identity[:], table_sb[:].indirect(pieces[p]), start=True, stop=True)
-        for p in range(PIECES):
-            for b in range(BLOCKS):
+        for b in range(BLOCKS):
+            for p in range(PIECES):
                 nc.tensor.matmul(
                     bank[b][:, p * PIECE : (p + 1) * PIECE],
-                    w_sb[:, b * P : (b + 1) * P],
+                    w_sb[b][:],
                     table_sb[:].indirect(pieces[p]),
                     start=True,
                     stop=True,
@@ -72,13 +76,17 @@ def tile_model_kernel(tc, table, w, offs, out):
         for p in range(PIECES):
             nc.scalar.activation(tail_sq[:, p * PIECE : (p + 1) * PIECE], picked[p][:], FUNC.Square)
         head_inv = held.tile([P, BLOCKS], F32, name="head_inv")
-        nc.scalar.activation(head_inv[:], head_sq[:], FUNC.Abs_reciprocal_sqrt)
+        nc.scalar.activation(head_inv[:, 0:1], head_sq[:], FUNC.Abs_reciprocal_sqrt)
 
         tail_inv = [held.tile([P, part.stop - part.start], F32, name=f"tail_inv{q}") for q, part in enumerate(PARTS)]
         for q, part in enumerate(PARTS):
             sums = psum.tile([P, part.stop - part.start], F32, name=f"sums{q}")
             nc.tensor.matmul(sums[:], ones[:], tail_sq[:, part], start=True, stop=True)
             nc.scalar.activation(tail_inv[q][:], sums[:], FUNC.Abs_reciprocal_sqrt)
+            if q == 0:
+                norms_1 = bank[1][:, N + HALF : N + HALF + 1]
+                nc.tensor.matmul(norms_1, w_sq[:], ones[:, 0:1], start=True, stop=True)
+                nc.scalar.activation(head_inv[:, 1:2], norms_1, FUNC.Abs_reciprocal_sqrt)
         for q, part in enumerate(PARTS):
             for b in range(BLOCKS):
                 cos = held.tile([P, part.stop - part.start], F32, name=f"cos{q}_{b}")

@@ -9,7 +9,6 @@ BLOCKS = M // P
 PIECE = 192
 PIECES = N // PIECE
 PIECE_COLS = PIECE // 16
-HALF = P // 2
 BANK = 512
 FIRST = N // 3
 PARTS = [slice(0, FIRST), slice(FIRST, N)]
@@ -19,7 +18,7 @@ BF16, F32, U16 = mybir.dt.bfloat16, mybir.dt.float32, mybir.dt.uint16
 FUNC = mybir.ActivationFunctionType
 MULT = mybir.AluOpType.mult
 
-assert N + HALF < BANK
+assert N + FIRST == BANK
 
 
 def tile_model_kernel(tc, table, w, offs, out):
@@ -28,13 +27,13 @@ def tile_model_kernel(tc, table, w, offs, out):
         tc.tile_pool(name="held", bufs=1) as held,
         tc.psum_pool(name="psum", bufs=1) as psum,
     ):
-        w_sb = [held.tile([P, P], BF16, name=f"w_sb{b}") for b in range(BLOCKS)]
-        nc.sync.dma_start(w_sb[0][:], w[:, :P])
+        w_loaded = [held.tile([P, P], BF16, name=f"w_loaded{b}") for b in range(BLOCKS)]
+        nc.sync.dma_start(w_loaded[0][:], w[:, :P])
         table_sb = held.tile([P, S], BF16, name="table_sb")
         nc.scalar.dma_start(table_sb[:], table)
         offsets = held.tile([P, N // 16], U16, name="offsets")
         nc.sync.dma_start(offsets[:], offs)
-        nc.scalar.dma_start(w_sb[1][:], w[:, P:])
+        nc.scalar.dma_start(w_loaded[1][:], w[:, P:])
 
         ones = held.tile([P, P], BF16, name="ones")
         nc.vector.memset(ones[:], 1.0)
@@ -44,19 +43,16 @@ def tile_model_kernel(tc, table, w, offs, out):
         unused_sb = held.tile([P, 1], F32, name="unused_sb")
         nc.scalar.activation(unused_sb[:], ones[:, 0:1], FUNC.Abs_reciprocal_sqrt)
 
-        bank = [psum.tile([P, BANK], F32, name=f"bank{b}") for b in range(BLOCKS)]
+        one = held.tile([P, 1], F32, name="one")
+        nc.vector.reduce_sum(one[:], identity[:], axis=mybir.AxisListType.X)
+        w_sb = [held.tile([P, P], BF16, name=f"w_sb{b}") for b in range(BLOCKS)]
+        w_sq = [held.tile([P, P], BF16, name=f"w_sq{b}") for b in range(BLOCKS)]
+        for b in range(BLOCKS):
+            nc.vector.tensor_scalar(w_sb[b][:], w_loaded[b][:], one[:, 0:1], None, MULT)
+        for b in range(BLOCKS):
+            nc.vector.tensor_tensor(w_sq[b][:], w_sb[b][:], w_sb[b][:], MULT)
 
-        diagonal = held.tile([P, P], F32, name="diagonal")
-        for b in range(BLOCKS):
-            half = slice(b * HALF, (b + 1) * HALF)
-            nc.tensor.matmul(bank[b][:, N : N + HALF], w_sb[0][:], w_sb[0][:, half], start=True, stop=True)
-        for b in range(BLOCKS):
-            half = slice(b * HALF, (b + 1) * HALF)
-            nc.vector.tensor_tensor(diagonal[:, half], bank[b][:, N : N + HALF], identity[:, half], MULT)
-        head_sq = held.tile([P, 1], F32, name="head_sq")
-        nc.vector.reduce_sum(head_sq[:], diagonal[:], axis=mybir.AxisListType.X)
-        w_sq = held.tile([P, P], BF16, name="w_sq")
-        nc.gpsimd.tensor_tensor(w_sq[:], w_sb[1][:], w_sb[1][:], MULT)
+        bank = [psum.tile([P, BANK], F32, name=f"bank{b}") for b in range(BLOCKS)]
 
         pieces = [offsets[:, p * PIECE_COLS : (p + 1) * PIECE_COLS] for p in range(PIECES)]
         picked = [psum.tile([P, PIECE], F32, name=f"picked{p}") for p in range(PIECES)]
@@ -75,18 +71,19 @@ def tile_model_kernel(tc, table, w, offs, out):
         tail_sq = held.tile([P, N], BF16, name="tail_sq")
         for p in range(PIECES):
             nc.scalar.activation(tail_sq[:, p * PIECE : (p + 1) * PIECE], picked[p][:], FUNC.Square)
-        head_inv = held.tile([P, BLOCKS], F32, name="head_inv")
-        nc.scalar.activation(head_inv[:, 0:1], head_sq[:], FUNC.Abs_reciprocal_sqrt)
 
+        rest_sums = psum.tile([P, N - FIRST], F32, name="rest_sums")
+        tail_sums = [bank[0][:, N : N + FIRST], rest_sums[:]]
+        head_sums = bank[1][:, N : N + BLOCKS]
         tail_inv = [held.tile([P, part.stop - part.start], F32, name=f"tail_inv{q}") for q, part in enumerate(PARTS)]
+        head_inv = held.tile([P, BLOCKS], F32, name="head_inv")
         for q, part in enumerate(PARTS):
-            sums = psum.tile([P, part.stop - part.start], F32, name=f"sums{q}")
-            nc.tensor.matmul(sums[:], ones[:], tail_sq[:, part], start=True, stop=True)
-            nc.scalar.activation(tail_inv[q][:], sums[:], FUNC.Abs_reciprocal_sqrt)
+            nc.tensor.matmul(tail_sums[q], ones[:], tail_sq[:, part], start=True, stop=True)
+            nc.scalar.activation(tail_inv[q][:], tail_sums[q], FUNC.Abs_reciprocal_sqrt)
             if q == 0:
-                norms_1 = bank[1][:, N + HALF : N + HALF + 1]
-                nc.tensor.matmul(norms_1, w_sq[:], ones[:, 0:1], start=True, stop=True)
-                nc.scalar.activation(head_inv[:, 1:2], norms_1, FUNC.Abs_reciprocal_sqrt)
+                for b in range(BLOCKS):
+                    nc.tensor.matmul(head_sums[:, b : b + 1], w_sq[b][:], ones[:, 0:1], start=True, stop=True)
+                nc.scalar.activation(head_inv[:], head_sums, FUNC.Abs_reciprocal_sqrt)
         for q, part in enumerate(PARTS):
             for b in range(BLOCKS):
                 cos = held.tile([P, part.stop - part.start], F32, name=f"cos{q}_{b}")

import concourse.mybir as mybir
from concourse.masks import make_identity

P = 128
S = 256
M = 256
N = 384
BLOCKS = M // P
PIECE = 192
PIECES = N // PIECE
PIECE_COLS = PIECE // 16
BANK = 512
FIRST = N // 3
PARTS = [slice(0, FIRST), slice(FIRST, N)]
FLOPS = 2 * P * M * N

BF16, F32, U16 = mybir.dt.bfloat16, mybir.dt.float32, mybir.dt.uint16
FUNC = mybir.ActivationFunctionType
MULT = mybir.AluOpType.mult

assert N + FIRST == BANK


def tile_model_kernel(tc, table, w, offs, out):
    nc = tc.nc
    with (
        tc.tile_pool(name="held", bufs=1) as held,
        tc.psum_pool(name="psum", bufs=1) as psum,
    ):
        w_loaded = [held.tile([P, P], BF16, name=f"w_loaded{b}") for b in range(BLOCKS)]
        nc.sync.dma_start(w_loaded[0][:], w[:, :P])
        table_sb = held.tile([P, S], BF16, name="table_sb")
        nc.scalar.dma_start(table_sb[:], table)
        offsets = held.tile([P, N // 16], U16, name="offsets")
        nc.sync.dma_start(offsets[:], offs)
        nc.scalar.dma_start(w_loaded[1][:], w[:, P:])

        ones = held.tile([P, P], BF16, name="ones")
        nc.vector.memset(ones[:], 1.0)
        identity = held.tile([P, P], BF16, name="identity")
        make_identity(nc, identity[:])

        unused_sb = held.tile([P, 1], F32, name="unused_sb")
        nc.scalar.activation(unused_sb[:], ones[:, 0:1], FUNC.Abs_reciprocal_sqrt)

        one = held.tile([P, 1], F32, name="one")
        nc.vector.reduce_sum(one[:], identity[:], axis=mybir.AxisListType.X)
        w_sb = [held.tile([P, P], BF16, name=f"w_sb{b}") for b in range(BLOCKS)]
        w_sq = [held.tile([P, P], BF16, name=f"w_sq{b}") for b in range(BLOCKS)]
        for b in range(BLOCKS):
            nc.vector.tensor_scalar(w_sb[b][:], w_loaded[b][:], one[:, 0:1], None, MULT)
        for b in range(BLOCKS):
            nc.vector.tensor_tensor(w_sq[b][:], w_sb[b][:], w_sb[b][:], MULT)

        bank = [psum.tile([P, BANK], F32, name=f"bank{b}") for b in range(BLOCKS)]

        pieces = [offsets[:, p * PIECE_COLS : (p + 1) * PIECE_COLS] for p in range(PIECES)]
        picked = [psum.tile([P, PIECE], F32, name=f"picked{p}") for p in range(PIECES)]
        for p in range(PIECES):
            nc.tensor.matmul(picked[p][:], identity[:], table_sb[:].indirect(pieces[p]), start=True, stop=True)
        for b in range(BLOCKS):
            for p in range(PIECES):
                nc.tensor.matmul(
                    bank[b][:, p * PIECE : (p + 1) * PIECE],
                    w_sb[b][:],
                    table_sb[:].indirect(pieces[p]),
                    start=True,
                    stop=True,
                )

        tail_sq = held.tile([P, N], BF16, name="tail_sq")
        for p in range(PIECES):
            nc.scalar.activation(tail_sq[:, p * PIECE : (p + 1) * PIECE], picked[p][:], FUNC.Square)

        rest_sums = psum.tile([P, N - FIRST], F32, name="rest_sums")
        tail_sums = [bank[0][:, N : N + FIRST], rest_sums[:]]
        head_sums = bank[1][:, N : N + BLOCKS]
        tail_inv = [held.tile([P, part.stop - part.start], F32, name=f"tail_inv{q}") for q, part in enumerate(PARTS)]
        head_inv = held.tile([P, BLOCKS], F32, name="head_inv")
        for q, part in enumerate(PARTS):
            nc.tensor.matmul(tail_sums[q], ones[:], tail_sq[:, part], start=True, stop=True)
            nc.scalar.activation(tail_inv[q][:], tail_sums[q], FUNC.Abs_reciprocal_sqrt)
            if q == 0:
                for b in range(BLOCKS):
                    nc.tensor.matmul(head_sums[:, b : b + 1], w_sq[b][:], ones[:, 0:1], start=True, stop=True)
                nc.scalar.activation(head_inv[:], head_sums, FUNC.Abs_reciprocal_sqrt)
        for q, part in enumerate(PARTS):
            for b in range(BLOCKS):
                cos = held.tile([P, part.stop - part.start], F32, name=f"cos{q}_{b}")
                nc.vector.scalar_tensor_tensor(
                    cos[:], bank[b][:, part], head_inv[:, b : b + 1], tail_inv[q][:], MULT, MULT
                )
                nc.sync.dma_start(out[b * P : (b + 1) * P, part], cos[:])
